import numpy as np
import ml_dtypes


def mxq(x, axis, fmt="e4m3"):
    dtype, down = {"e4m3": (ml_dtypes.float8_e4m3fn, 7), "e5m2": (ml_dtypes.float8_e5m2, 14)}[fmt]
    v = np.moveaxis(np.asarray(x, np.float32).astype(ml_dtypes.bfloat16).astype(np.float64), axis, -1)
    blocks = v.reshape(v.shape[:-1] + (-1, 32))
    amax = np.abs(blocks).max(-1, keepdims=True)
    byte = np.maximum(np.where(amax > 0, np.frexp(amax)[1] - 1 + 127, 0) - down, 1)
    scale = np.exp2(byte - 127.0)
    codes = (blocks / scale).astype(np.float32).astype(dtype).astype(np.float64)
    return np.moveaxis((codes * scale).reshape(v.shape), -1, axis)


WIDE = False


def mx_kscale(k):
    if not WIDE:
        return np.ones(k)
    levels = np.array([10, -10, 5, -5, 0])
    a = np.random.permutation(np.resize(levels, k // 512 * 4)).reshape(k // 512, 4)
    idx = np.arange(k)
    return np.exp2(a[idx // 512, idx % 128 // 32])


BF16 = ml_dtypes.bfloat16


def bf(x):
    return np.asarray(x, np.float32).astype(BF16)


def f64(x):
    return np.asarray(x).astype(np.float64)


B, L, D, H = 1, 1024, 512, 8
LN_EPS = 1e-5


def setup_inputs():
    s = mx_kscale(H * D)
    return {"heads": bf(np.random.standard_normal((H, L, D)) * 0.25 * s.reshape(H, D)[:, None, :]),
            "q": bf(np.random.standard_normal((B, L, D))),
            "proj_w": bf(np.random.standard_normal((D, H * D)) * 4.0 / np.sqrt(H * D) / s[None, :]),
            "proj_b": bf(np.random.standard_normal(D) * 0.1),
            "ln_gamma": bf(1.0 + np.random.standard_normal(D) * 0.1),
            "ln_beta": bf(np.random.standard_normal(D) * 0.1)}


def reference(heads, q, proj_w, proj_b, ln_gamma, ln_beta):
    hc = f64(heads).transpose(1, 0, 2).reshape(B, L, H * D)
    o = (mxq(hc, 2, "e4m3") @ mxq(f64(proj_w), 1, "e4m3").T) + f64(proj_b)
    x = o + f64(q)
    mu = x.mean(-1, keepdims=True)
    var = ((x - mu) ** 2).mean(-1, keepdims=True)
    return (x - mu) / np.sqrt(var + LN_EPS) * f64(ln_gamma) + f64(ln_beta)

@@ -1,0 +1,253 @@
+from contextlib import ExitStack
+
+import concourse.mybir as mybir
+from concourse.masks import make_identity
+
+FLOPS = 2 * 1024 * 4096 * 512
+
+F32 = mybir.dt.float32
+BF16 = mybir.dt.bfloat16
+U32 = mybir.dt.uint32
+U8 = mybir.dt.uint8
+FP8X4 = mybir.dt.float8_e4m3fn_x4
+ADD = mybir.AluOpType.add
+MULT = mybir.AluOpType.mult
+SQUARE = mybir.ActivationFunctionType.Square
+SQRT = mybir.ActivationFunctionType.Sqrt
+
+P = 128
+HEADS = 8
+ROWS = 1024
+FEAT = 512
+LN_EPS = 1e-5
+
+STRIP_WORDS = FEAT // 2
+STRIPS = 8
+BANK_STRIPS = 2
+QUANT_STRIPS = 4
+TILES = 2
+GROUPS = ROWS // (TILES * P)
+X_HEADS = STRIPS // TILES
+X_CHUNKS = HEADS // X_HEADS
+W_BLOCKS = FEAT // P
+W_HEADS = STRIPS // W_BLOCKS
+W_CHUNKS = HEADS // W_HEADS
+
+
+def tile_multiheadattention_pb_kernel(tc, heads, q, proj_w, proj_b, ln_gamma, ln_beta, out):
+    nc = tc.nc
+    q_rows = q.flatten_outer_dims()
+    out_rows = out.flatten_outer_dims()
+
+    with ExitStack() as ctx:
+        ctx.enter_context(tc.manual_schedule())
+        const = ctx.enter_context(tc.tile_pool(name="const", bufs=1))
+        raw = ctx.enter_context(tc.tile_pool(name="raw", bufs=1))
+        stage = ctx.enter_context(tc.tile_pool(name="stage", bufs=3))
+        operands = ctx.enter_context(tc.tile_pool(name="operands", bufs=3))
+        rows_pool = ctx.enter_context(tc.tile_pool(name="rows", bufs=4))
+        stats = ctx.enter_context(tc.tile_pool(name="stats", bufs=4))
+        banks = ctx.enter_context(tc.psum_pool(name="banks", bufs=4))
+        sums = ctx.enter_context(tc.psum_pool(name="sums", bufs=4))
+
+        ident = const.tile([P, P], F32)
+        make_identity(nc, ident[:])
+        ones = const.tile([P, P], BF16)
+        nc.vector.memset(ones[:], 1.0)
+        eps = const.tile([P, 1], F32)
+        nc.vector.memset(eps[:], LN_EPS)
+        vector_rows = const.tile([P, 3, FEAT], BF16)
+        nc.vector.memset(vector_rows[:], 0.0)
+        for j, vector in enumerate((proj_b, ln_gamma, ln_beta)):
+            nc.scalar.dma_start(out=vector_rows[0:1, j, :], in_=vector.rearrange("(o n) -> o n", o=1))
+        warm = const.tile([P, 1], F32)
+        nc.scalar.activation(out=warm[:], in_=eps[:], func=SQRT)
+
+        w_raw = []
+        x_raw = {}
+        q_raw = []
+
+        def load_w(c):
+            w_chunk = raw.tile([P, W_BLOCKS * W_HEADS * FEAT], BF16, name="w_raw%d" % c)
+            nc.sync.dma_start(
+                out=w_chunk[:].rearrange("p (b k) -> p b k", b=W_BLOCKS),
+                in_=proj_w[:, c * W_HEADS * FEAT : (c + 1) * W_HEADS * FEAT].rearrange("(b p) k -> p b k", p=P),
+            )
+            w_raw.append(w_chunk)
+
+        def load_x(g, c):
+            x_chunk = raw.tile([P, X_HEADS * TILES * FEAT], BF16, name="x_raw%d_%d" % (g, c))
+            nc.sync.dma_start(
+                out=x_chunk[:].rearrange("p (h r) -> p h r", h=X_HEADS),
+                in_=heads[c * X_HEADS : (c + 1) * X_HEADS, g * TILES * P : (g + 1) * TILES * P, :].rearrange(
+                    "h (p t) d -> p h (t d)", t=TILES
+                ),
+            )
+            x_raw[(g, c)] = x_chunk
+
+        def load_q(g):
+            q_group = raw.tile([P, TILES * FEAT], BF16, name="q_raw%d" % g)
+            nc.sync.dma_start(
+                out=q_group[:],
+                in_=q_rows[g * TILES * P : (g + 1) * TILES * P, :].rearrange("(p t) n -> p (t n)", t=TILES),
+            )
+            q_raw.append(q_group)
+
+        for c in range(X_CHUNKS):
+            load_w(2 * c)
+            load_w(2 * c + 1)
+            load_x(0, c)
+        load_q(0)
+        for g in range(1, GROUPS):
+            for c in range(X_CHUNKS):
+                load_x(g, c)
+            load_q(g)
+
+        bias_all = const.tile([P, FEAT], F32)
+        gamma_all = const.tile([P, FEAT], F32)
+        beta_all = const.tile([P, FEAT], F32)
+
+        def spread_vectors():
+            for j, spread in enumerate((bias_all, gamma_all, beta_all)):
+                bank = banks.tile([P, FEAT], F32, tag="bank")
+                nc.tensor.matmul(out=bank[:], lhsT=ones[:], rhs=vector_rows[:, j, :], start=True, stop=True)
+                nc.vector.tensor_copy(out=spread[:], in_=bank[:])
+
+        w_codes = const.tile([P, HEADS * FEAT], U32, align_bytes=64)
+        w_scales = const.tile([P, HEADS * FEAT], U8, align_bytes=64)
+        x_operands = {}
+        acc = {}
+        residual = {}
+        centred = {}
+
+        def prepare(strips, codes, scales):
+            grouped = stage.tile([P, STRIPS * FEAT], BF16, align_bytes=64)
+            grouped_words = grouped[:].bitcast(F32).rearrange("p (s r u) -> p s r u", s=STRIPS, u=2)
+            for b in range(STRIPS // BANK_STRIPS):
+                bank = banks.tile([P, FEAT], F32, tag="bank")
+                halves = bank[:].rearrange("p (a u r) -> p a u r", a=BANK_STRIPS, u=2)
+                for a in range(BANK_STRIPS):
+                    for u in range(2):
+                        nc.tensor.transpose(
+                            halves[:, a, u, :], strips[b * BANK_STRIPS + a][:, u * P : (u + 1) * P], ident[:]
+                        )
+                nc.scalar.copy(
+                    out=grouped_words[:, b * BANK_STRIPS : (b + 1) * BANK_STRIPS, :, :],
+                    in_=bank[:].rearrange("p (a u r) -> p a r u", a=BANK_STRIPS, u=2),
+                )
+            for s in range(0, STRIPS, QUANT_STRIPS):
+                nc.vector.quantize_mx(
+                    out=codes[:, s * P : (s + QUANT_STRIPS) * P].bitcast(FP8X4),
+                    scales=scales[:, s * P : (s + QUANT_STRIPS) * P],
+                    in_=grouped[:, s * FEAT : (s + QUANT_STRIPS) * FEAT],
+                )
+
+        def prepare_w(c):
+            words = w_raw[c][:].bitcast(F32)
+            strips = [
+                words[:, (b * W_HEADS + h) * STRIP_WORDS : (b * W_HEADS + h + 1) * STRIP_WORDS]
+                for h in range(W_HEADS)
+                for b in range(W_BLOCKS)
+            ]
+            columns = slice(c * STRIPS * P, (c + 1) * STRIPS * P)
+            prepare(strips, w_codes[:, columns], w_scales[:, columns])
+
+        def prepare_x(g, c):
+            words = x_raw[(g, c)][:].bitcast(F32)
+            strips = [words[:, s * STRIP_WORDS : (s + 1) * STRIP_WORDS] for s in range(STRIPS)]
+            x_codes = operands.tile([P, STRIPS * P], U32, align_bytes=64)
+            x_scales = operands.tile([P, STRIPS * P], U8, align_bytes=64)
+            prepare(strips, x_codes[:], x_scales[:])
+            x_operands[(g, c)] = (x_codes, x_scales)
+
+        def multiply(g, c):
+            x_codes, x_scales = x_operands[(g, c)]
+            for t in range(TILES):
+                if c == 0:
+                    acc[(g, t)] = sums.tile([P, FEAT], F32, name="acc", tag="acc")
+                for h in range(X_HEADS):
+                    head = c * X_HEADS + h
+                    strip = slice((h * TILES + t) * P, (h * TILES + t + 1) * P)
+                    nc.tensor.matmul_mx(
+                        out=acc[(g, t)][:],
+                        lhsT=x_codes[:, strip].bitcast(FP8X4),
+                        lhsT_scale=x_scales[:, strip],
+                        rhs=w_codes[:, head * FEAT : (head + 1) * FEAT].bitcast(FP8X4),
+                        rhs_scale=w_scales[:, head * FEAT : (head + 1) * FEAT],
+                        start=(head == 0),
+                        stop=(head == HEADS - 1),
+                    )
+
+        def add_bias_to_residual(g):
+            q_plus_b = rows_pool.tile([P, TILES, FEAT], F32, bufs=2)
+            nc.vector.tensor_tensor(
+                out=q_plus_b[:],
+                in0=q_raw[g][:].rearrange("p (t n) -> p t n", t=TILES),
+                in1=bias_all[:].unsqueeze(1).to_broadcast([P, TILES, FEAT]),
+                op=ADD,
+            )
+            residual[g] = q_plus_b
+
+        def centre(g):
+            for t in range(TILES):
+                x = rows_pool.tile([P, FEAT], F32)
+                row_sum = stats.tile([P, 1], F32)
+                nc.vector.scalar_tensor_tensor(
+                    out=x[:], in0=acc[(g, t)][:], scalar=0.0, in1=residual[g][:, t, :], op0=ADD, op1=ADD,
+                    accum_out=row_sum[:],
+                )
+                minus_mean = stats.tile([P, 1], F32)
+                nc.vector.tensor_scalar(
+                    out=minus_mean[:], in0=row_sum[:], scalar1=-1.0 / FEAT, scalar2=None, op0=MULT
+                )
+                centred[(g, t)] = (x, minus_mean)
+            for t in range(TILES):
+                x, minus_mean = centred[(g, t)]
+                scaled = rows_pool.tile([P, FEAT], F32)
+                nc.vector.scalar_tensor_tensor(
+                    out=scaled[:], in0=x[:], scalar=minus_mean[:], in1=gamma_all[:], op0=ADD, op1=MULT
+                )
+                centred[(g, t)] = (x, minus_mean, scaled)
+
+        def normalise_and_store(g):
+            group_rows = out_rows[g * TILES * P : (g + 1) * TILES * P, :].rearrange("(p t) n -> p t n", t=TILES)
+            deviations = []
+            for t in range(TILES):
+                x, minus_mean, scaled = centred[(g, t)]
+                squares = rows_pool.tile([P, FEAT], F32, bufs=2)
+                square_sum = stats.tile([P, 1], F32)
+                nc.scalar.activation(
+                    out=squares[:], in_=x[:], func=SQUARE, bias=minus_mean[:], scale=1.0, accum_out=square_sum[:]
+                )
+                deviation = stats.tile([P, 1], F32)
+                nc.scalar.activation(out=deviation[:], in_=square_sum[:], func=SQRT, bias=eps[:], scale=1.0 / FEAT)
+                deviations.append(deviation)
+            for t in range(TILES):
+                scaled = centred[(g, t)][2]
+                inverse = stats.tile([P, 1], F32)
+                nc.vector.reciprocal(out=inverse[:], in_=deviations[t][:])
+                nc.vector.scalar_tensor_tensor(
+                    out=scaled[:], in0=scaled[:], scalar=inverse[:], in1=beta_all[:], op0=MULT, op1=ADD
+                )
+                nc.sync.dma_start(out=group_rows[:, t, :], in_=scaled[:])
+
+        prepare_w(0)
+        prepare_w(1)
+        prepare_x(0, 0)
+        prepare_w(2)
+        multiply(0, 0)
+        prepare_w(3)
+        prepare_x(0, 1)
+        spread_vectors()
+        add_bias_to_residual(0)
+        for g in range(1, GROUPS):
+            prepare_x(g, 0)
+            multiply(g - 1, 1)
+            centre(g - 1)
+            prepare_x(g, 1)
+            normalise_and_store(g - 1)
+            add_bias_to_residual(g)
+            multiply(g, 0)
+        multiply(GROUPS - 1, 1)
+        centre(GROUPS - 1)
+        normalise_and_store(GROUPS - 1)

@@ -13,7 +13,7 @@ FP8X4 = mybir.dt.float8_e4m3fn_x4
 ADD = mybir.AluOpType.add
 MULT = mybir.AluOpType.mult
 SQUARE = mybir.ActivationFunctionType.Square
-SQRT = mybir.ActivationFunctionType.Sqrt
+INV_SQRT = mybir.ActivationFunctionType.Abs_reciprocal_sqrt
 
 P = 128
 HEADS = 8
@@ -61,7 +61,7 @@ def tile_multiheadattention_pb_kernel(tc, heads, q, proj_w, proj_b, ln_gamma, ln
         for j, vector in enumerate((proj_b, ln_gamma, ln_beta)):
             nc.scalar.dma_start(out=vector_rows[0:1, j, :], in_=vector.rearrange("(o n) -> o n", o=1))
         warm = const.tile([P, 1], F32)
-        nc.scalar.activation(out=warm[:], in_=eps[:], func=SQRT)
+        nc.scalar.activation(out=warm[:], in_=eps[:], func=INV_SQRT)
 
         w_raw = []
         x_raw = {}
@@ -99,9 +99,9 @@ def tile_multiheadattention_pb_kernel(tc, heads, q, proj_w, proj_b, ln_gamma, ln
             load_x(0, c)
         load_q(0)
         for g in range(1, GROUPS):
-            for c in range(X_CHUNKS):
-                load_x(g, c)
+            load_x(g, 0)
             load_q(g)
+            load_x(g, 1)
 
         bias_all = const.tile([P, FEAT], F32)
         gamma_all = const.tile([P, FEAT], F32)
@@ -188,7 +188,7 @@ def tile_multiheadattention_pb_kernel(tc, heads, q, proj_w, proj_b, ln_gamma, ln
             )
             residual[g] = q_plus_b
 
-        def centre(g):
+        def take_sums(g):
             for t in range(TILES):
                 x = rows_pool.tile([P, FEAT], F32)
                 row_sum = stats.tile([P, 1], F32)
@@ -197,10 +197,12 @@ def tile_multiheadattention_pb_kernel(tc, heads, q, proj_w, proj_b, ln_gamma, ln
                     accum_out=row_sum[:],
                 )
                 minus_mean = stats.tile([P, 1], F32)
-                nc.vector.tensor_scalar(
-                    out=minus_mean[:], in0=row_sum[:], scalar1=-1.0 / FEAT, scalar2=None, op0=MULT
+                nc.gpsimd.tensor_scalar(
+                    out=minus_mean[:], in0=row_sum[:], scalar1=-1.0 / FEAT, scalar2=0.0, op0=MULT, op1=ADD
                 )
                 centred[(g, t)] = (x, minus_mean)
+
+        def scale_by_gamma(g):
             for t in range(TILES):
                 x, minus_mean = centred[(g, t)]
                 scaled = rows_pool.tile([P, FEAT], F32)
@@ -211,7 +213,6 @@ def tile_multiheadattention_pb_kernel(tc, heads, q, proj_w, proj_b, ln_gamma, ln
 
         def normalise_and_store(g):
             group_rows = out_rows[g * TILES * P : (g + 1) * TILES * P, :].rearrange("(p t) n -> p t n", t=TILES)
-            deviations = []
             for t in range(TILES):
                 x, minus_mean, scaled = centred[(g, t)]
                 squares = rows_pool.tile([P, FEAT], F32, bufs=2)
@@ -219,13 +220,8 @@ def tile_multiheadattention_pb_kernel(tc, heads, q, proj_w, proj_b, ln_gamma, ln
                 nc.scalar.activation(
                     out=squares[:], in_=x[:], func=SQUARE, bias=minus_mean[:], scale=1.0, accum_out=square_sum[:]
                 )
-                deviation = stats.tile([P, 1], F32)
-                nc.scalar.activation(out=deviation[:], in_=square_sum[:], func=SQRT, bias=eps[:], scale=1.0 / FEAT)
-                deviations.append(deviation)
-            for t in range(TILES):
-                scaled = centred[(g, t)][2]
                 inverse = stats.tile([P, 1], F32)
-                nc.vector.reciprocal(out=inverse[:], in_=deviations[t][:])
+                nc.scalar.activation(out=inverse[:], in_=square_sum[:], func=INV_SQRT, bias=eps[:], scale=1.0 / FEAT)
                 nc.vector.scalar_tensor_tensor(
                     out=scaled[:], in0=scaled[:], scalar=inverse[:], in1=beta_all[:], op0=MULT, op1=ADD
                 )
@@ -243,11 +239,13 @@ def tile_multiheadattention_pb_kernel(tc, heads, q, proj_w, proj_b, ln_gamma, ln
         for g in range(1, GROUPS):
             prepare_x(g, 0)
             multiply(g - 1, 1)
-            centre(g - 1)
+            take_sums(g - 1)
+            add_bias_to_residual(g)
+            scale_by_gamma(g - 1)
             prepare_x(g, 1)
             normalise_and_store(g - 1)
-            add_bias_to_residual(g)
             multiply(g, 0)
         multiply(GROUPS - 1, 1)
-        centre(GROUPS - 1)
+        take_sums(GROUPS - 1)
+        scale_by_gamma(GROUPS - 1)
         normalise_and_store(GROUPS - 1)

@@ -21,17 +21,14 @@ ROWS = 1024
 FEAT = 512
 LN_EPS = 1e-5
 
-STRIP_WORDS = FEAT // 2
 STRIPS = 8
 BANK_STRIPS = 2
+PIECES = STRIPS // BANK_STRIPS
 QUANT_STRIPS = 4
 TILES = 2
 GROUPS = ROWS // (TILES * P)
 X_HEADS = STRIPS // TILES
-X_CHUNKS = HEADS // X_HEADS
-W_BLOCKS = FEAT // P
-W_HEADS = STRIPS // W_BLOCKS
-W_CHUNKS = HEADS // W_HEADS
+W_HEADS = STRIPS * P // FEAT
 
 
 def tile_multiheadattention_pb_kernel(tc, heads, q, proj_w, proj_b, ln_gamma, ln_beta, out):
@@ -68,22 +65,27 @@ def tile_multiheadattention_pb_kernel(tc, heads, q, proj_w, proj_b, ln_gamma, ln
         q_raw = []
 
         def load_w(c):
-            w_chunk = raw.tile([P, W_BLOCKS * W_HEADS * FEAT], BF16, name="w_raw%d" % c)
-            nc.sync.dma_start(
-                out=w_chunk[:].rearrange("p (b k) -> p b k", b=W_BLOCKS),
-                in_=proj_w[:, c * W_HEADS * FEAT : (c + 1) * W_HEADS * FEAT].rearrange("(b p) k -> p b k", p=P),
-            )
-            w_raw.append(w_chunk)
+            pieces = []
+            for b in range(PIECES):
+                piece = raw.tile([P, BANK_STRIPS * FEAT], BF16, name="w_raw%d_%d" % (c, b))
+                nc.sync.dma_start(
+                    out=piece[:], in_=proj_w[b * P : (b + 1) * P, c * W_HEADS * FEAT : (c + 1) * W_HEADS * FEAT]
+                )
+                pieces.append(piece)
+            w_raw.append(pieces)
 
         def load_x(g, c):
-            x_chunk = raw.tile([P, X_HEADS * TILES * FEAT], BF16, name="x_raw%d_%d" % (g, c))
-            nc.sync.dma_start(
-                out=x_chunk[:].rearrange("p (h r) -> p h r", h=X_HEADS),
-                in_=heads[c * X_HEADS : (c + 1) * X_HEADS, g * TILES * P : (g + 1) * TILES * P, :].rearrange(
-                    "h (p t) d -> p h (t d)", t=TILES
-                ),
-            )
-            x_raw[(g, c)] = x_chunk
+            pieces = []
+            for b in range(PIECES):
+                piece = raw.tile([P, BANK_STRIPS * FEAT], BF16, name="x_raw%d_%d_%d" % (g, c, b))
+                nc.sync.dma_start(
+                    out=piece[:],
+                    in_=heads[c * X_HEADS + b, g * TILES * P : (g + 1) * TILES * P, :].rearrange(
+                        "(p t) d -> p (t d)", t=TILES
+                    ),
+                )
+                pieces.append(piece)
+            x_raw[(g, c)] = pieces
 
         def load_q(g):
             q_group = raw.tile([P, TILES * FEAT], BF16, name="q_raw%d" % g)
@@ -93,14 +95,16 @@ def tile_multiheadattention_pb_kernel(tc, heads, q, proj_w, proj_b, ln_gamma, ln
             )
             q_raw.append(q_group)
 
-        for c in range(X_CHUNKS):
-            load_w(2 * c)
-            load_w(2 * c + 1)
-            load_x(0, c)
+        load_w(0)
+        load_x(0, 0)
+        load_w(1)
+        load_w(2)
+        load_x(0, 1)
+        load_w(3)
         load_q(0)
         for g in range(1, GROUPS):
-            load_x(g, 0)
             load_q(g)
+            load_x(g, 0)
             load_x(g, 1)
 
         bias_all = const.tile([P, FEAT], F32)
@@ -116,25 +120,20 @@ def tile_multiheadattention_pb_kernel(tc, heads, q, proj_w, proj_b, ln_gamma, ln
         w_codes = const.tile([P, HEADS * FEAT], U32, align_bytes=64)
         w_scales = const.tile([P, HEADS * FEAT], U8, align_bytes=64)
         x_operands = {}
+        heads_done = [0] * GROUPS
         acc = {}
         residual = {}
         centred = {}
 
-        def prepare(strips, codes, scales):
+        def prepare(pieces, order, codes, scales):
             grouped = stage.tile([P, STRIPS * FEAT], BF16, align_bytes=64)
-            grouped_words = grouped[:].bitcast(F32).rearrange("p (s r u) -> p s r u", s=STRIPS, u=2)
-            for b in range(STRIPS // BANK_STRIPS):
+            places = grouped[:].bitcast(F32).rearrange(order, a=BANK_STRIPS, b=PIECES, u=2)
+            for b in range(PIECES):
+                words = pieces[b][:].bitcast(F32)
                 bank = banks.tile([P, FEAT], F32, tag="bank")
-                halves = bank[:].rearrange("p (a u r) -> p a u r", a=BANK_STRIPS, u=2)
-                for a in range(BANK_STRIPS):
-                    for u in range(2):
-                        nc.tensor.transpose(
-                            halves[:, a, u, :], strips[b * BANK_STRIPS + a][:, u * P : (u + 1) * P], ident[:]
-                        )
-                nc.scalar.copy(
-                    out=grouped_words[:, b * BANK_STRIPS : (b + 1) * BANK_STRIPS, :, :],
-                    in_=bank[:].rearrange("p (a u r) -> p a r u", a=BANK_STRIPS, u=2),
-                )
+                for j in range(BANK_STRIPS * 2):
+                    nc.tensor.transpose(bank[:, j * P : (j + 1) * P], words[:, j * P : (j + 1) * P], ident[:])
+                nc.scalar.copy(out=places[:, b, :, :, :], in_=bank[:].rearrange("p (a u r) -> p a r u", a=BANK_STRIPS, u=2))
             for s in range(0, STRIPS, QUANT_STRIPS):
                 nc.vector.quantize_mx(
                     out=codes[:, s * P : (s + QUANT_STRIPS) * P].bitcast(FP8X4),
@@ -143,40 +142,32 @@ def tile_multiheadattention_pb_kernel(tc, heads, q, proj_w, proj_b, ln_gamma, ln
                 )
 
         def prepare_w(c):
-            words = w_raw[c][:].bitcast(F32)
-            strips = [
-                words[:, (b * W_HEADS + h) * STRIP_WORDS : (b * W_HEADS + h + 1) * STRIP_WORDS]
-                for h in range(W_HEADS)
-                for b in range(W_BLOCKS)
-            ]
             columns = slice(c * STRIPS * P, (c + 1) * STRIPS * P)
-            prepare(strips, w_codes[:, columns], w_scales[:, columns])
+            prepare(w_raw[c], "p (a b r u) -> p b a r u", w_codes[:, columns], w_scales[:, columns])
 
         def prepare_x(g, c):
-            words = x_raw[(g, c)][:].bitcast(F32)
-            strips = [words[:, s * STRIP_WORDS : (s + 1) * STRIP_WORDS] for s in range(STRIPS)]
             x_codes = operands.tile([P, STRIPS * P], U32, align_bytes=64)
             x_scales = operands.tile([P, STRIPS * P], U8, align_bytes=64)
-            prepare(strips, x_codes[:], x_scales[:])
+            prepare(x_raw[(g, c)], "p (b a r u) -> p b a r u", x_codes[:], x_scales[:])
             x_operands[(g, c)] = (x_codes, x_scales)
 
-        def multiply(g, c):
-            x_codes, x_scales = x_operands[(g, c)]
+        def multiply(g, end):
             for t in range(TILES):
-                if c == 0:
+                if heads_done[g] == 0:
                     acc[(g, t)] = sums.tile([P, FEAT], F32, name="acc", tag="acc")
-                for h in range(X_HEADS):
-                    head = c * X_HEADS + h
-                    strip = slice((h * TILES + t) * P, (h * TILES + t + 1) * P)
+                for head in range(heads_done[g], end):
+                    x_codes, x_scales = x_operands[(g, head // X_HEADS)]
+                    strip = (head % X_HEADS) * TILES + t
                     nc.tensor.matmul_mx(
                         out=acc[(g, t)][:],
-                        lhsT=x_codes[:, strip].bitcast(FP8X4),
-                        lhsT_scale=x_scales[:, strip],
+                        lhsT=x_codes[:, strip * P : (strip + 1) * P].bitcast(FP8X4),
+                        lhsT_scale=x_scales[:, strip * P : (strip + 1) * P],
                         rhs=w_codes[:, head * FEAT : (head + 1) * FEAT].bitcast(FP8X4),
                         rhs_scale=w_scales[:, head * FEAT : (head + 1) * FEAT],
                         start=(head == 0),
                         stop=(head == HEADS - 1),
                     )
+            heads_done[g] = end
 
         def add_bias_to_residual(g):
             q_plus_b = rows_pool.tile([P, TILES, FEAT], F32, bufs=2)
@@ -228,24 +219,26 @@ def tile_multiheadattention_pb_kernel(tc, heads, q, proj_w, proj_b, ln_gamma, ln
                 nc.sync.dma_start(out=group_rows[:, t, :], in_=scaled[:])
 
         prepare_w(0)
-        prepare_w(1)
         prepare_x(0, 0)
+        prepare_w(1)
+        multiply(0, W_HEADS)
         prepare_w(2)
-        multiply(0, 0)
-        prepare_w(3)
+        multiply(0, 2 * W_HEADS)
         prepare_x(0, 1)
         spread_vectors()
+        prepare_w(3)
+        multiply(0, 3 * W_HEADS)
         add_bias_to_residual(0)
         for g in range(1, GROUPS):
-            prepare_x(g, 0)
-            multiply(g - 1, 1)
-            take_sums(g - 1)
             add_bias_to_residual(g)
-            scale_by_gamma(g - 1)
+            prepare_x(g, 0)
+            multiply(g - 1, HEADS)
+            take_sums(g - 1)
             prepare_x(g, 1)
+            scale_by_gamma(g - 1)
             normalise_and_store(g - 1)
-            multiply(g, 0)
-        multiply(GROUPS - 1, 1)
+            multiply(g, X_HEADS)
+        multiply(GROUPS - 1, HEADS)
         take_sums(GROUPS - 1)
         scale_by_gamma(GROUPS - 1)
         normalise_and_store(GROUPS - 1)

@@ -21,14 +21,15 @@ ROWS = 1024
 FEAT = 512
 LN_EPS = 1e-5
 
-STRIPS = 8
-BANK_STRIPS = 2
-PIECES = STRIPS // BANK_STRIPS
-QUANT_STRIPS = 4
+PIECE_STRIPS = 2
+STEP_PIECES = 2
+STEP_STRIPS = STEP_PIECES * PIECE_STRIPS
 TILES = 2
 GROUPS = ROWS // (TILES * P)
-X_HEADS = STRIPS // TILES
-W_HEADS = STRIPS * P // FEAT
+PAIR = 2
+PAIRS = HEADS // PAIR
+W_BLOCKS = FEAT // P
+W_STEPS = W_BLOCKS // STEP_PIECES
 
 
 def tile_multiheadattention_pb_kernel(tc, heads, q, proj_w, proj_b, ln_gamma, ln_beta, out):
@@ -40,12 +41,13 @@ def tile_multiheadattention_pb_kernel(tc, heads, q, proj_w, proj_b, ln_gamma, ln
         ctx.enter_context(tc.manual_schedule())
         const = ctx.enter_context(tc.tile_pool(name="const", bufs=1))
         raw = ctx.enter_context(tc.tile_pool(name="raw", bufs=1))
-        stage = ctx.enter_context(tc.tile_pool(name="stage", bufs=3))
-        operands = ctx.enter_context(tc.tile_pool(name="operands", bufs=3))
+        stage = ctx.enter_context(tc.tile_pool(name="stage", bufs=6))
+        operands = ctx.enter_context(tc.tile_pool(name="operands", bufs=6))
         rows_pool = ctx.enter_context(tc.tile_pool(name="rows", bufs=4))
         stats = ctx.enter_context(tc.tile_pool(name="stats", bufs=4))
         banks = ctx.enter_context(tc.psum_pool(name="banks", bufs=4))
-        sums = ctx.enter_context(tc.psum_pool(name="sums", bufs=4))
+        sums = ctx.enter_context(tc.psum_pool(name="sums", bufs=3))
+        spread_pool = ctx.enter_context(tc.psum_pool(name="spread", bufs=1))
 
         ident = const.tile([P, P], F32)
         make_identity(nc, ident[:])
@@ -60,32 +62,28 @@ def tile_multiheadattention_pb_kernel(tc, heads, q, proj_w, proj_b, ln_gamma, ln
         warm = const.tile([P, 1], F32)
         nc.scalar.activation(out=warm[:], in_=eps[:], func=INV_SQRT)
 
-        w_raw = []
+        w_raw = {}
         x_raw = {}
         q_raw = []
 
-        def load_w(c):
-            pieces = []
-            for b in range(PIECES):
-                piece = raw.tile([P, BANK_STRIPS * FEAT], BF16, name="w_raw%d_%d" % (c, b))
+        def load_w(pair):
+            for b in range(W_BLOCKS):
+                piece = raw.tile([P, PIECE_STRIPS * FEAT], BF16, name="w_raw%d_%d" % (pair, b))
                 nc.sync.dma_start(
-                    out=piece[:], in_=proj_w[b * P : (b + 1) * P, c * W_HEADS * FEAT : (c + 1) * W_HEADS * FEAT]
+                    out=piece[:], in_=proj_w[b * P : (b + 1) * P, pair * PAIR * FEAT : (pair + 1) * PAIR * FEAT]
                 )
-                pieces.append(piece)
-            w_raw.append(pieces)
+                w_raw[(pair, b)] = piece
 
-        def load_x(g, c):
-            pieces = []
-            for b in range(PIECES):
-                piece = raw.tile([P, BANK_STRIPS * FEAT], BF16, name="x_raw%d_%d_%d" % (g, c, b))
+        def load_x(g, pair):
+            for b in range(PAIR):
+                piece = raw.tile([P, PIECE_STRIPS * FEAT], BF16, name="x_raw%d_%d_%d" % (g, pair, b))
                 nc.sync.dma_start(
                     out=piece[:],
-                    in_=heads[c * X_HEADS + b, g * TILES * P : (g + 1) * TILES * P, :].rearrange(
+                    in_=heads[pair * PAIR + b, g * TILES * P : (g + 1) * TILES * P, :].rearrange(
                         "(p t) d -> p (t d)", t=TILES
                     ),
                 )
-                pieces.append(piece)
-            x_raw[(g, c)] = pieces
+                x_raw[(g, pair, b)] = piece
 
         def load_q(g):
             q_group = raw.tile([P, TILES * FEAT], BF16, name="q_raw%d" % g)
@@ -97,25 +95,26 @@ def tile_multiheadattention_pb_kernel(tc, heads, q, proj_w, proj_b, ln_gamma, ln
 
         load_w(0)
         load_x(0, 0)
+        load_x(0, 1)
         load_w(1)
         load_w(2)
-        load_x(0, 1)
+        load_x(0, 2)
+        load_x(0, 3)
         load_w(3)
         load_q(0)
         for g in range(1, GROUPS):
             load_q(g)
-            load_x(g, 0)
-            load_x(g, 1)
+            for pair in range(PAIRS):
+                load_x(g, pair)
 
         bias_all = const.tile([P, FEAT], F32)
         gamma_all = const.tile([P, FEAT], F32)
         beta_all = const.tile([P, FEAT], F32)
 
-        def spread_vectors():
-            for j, spread in enumerate((bias_all, gamma_all, beta_all)):
-                bank = banks.tile([P, FEAT], F32, tag="bank")
-                nc.tensor.matmul(out=bank[:], lhsT=ones[:], rhs=vector_rows[:, j, :], start=True, stop=True)
-                nc.vector.tensor_copy(out=spread[:], in_=bank[:])
+        def spread_vector(j, everywhere):
+            repeated = spread_pool.tile([P, FEAT], F32)
+            nc.tensor.matmul(out=repeated[:], lhsT=ones[:], rhs=vector_rows[:, j, :], start=True, stop=True)
+            nc.vector.tensor_copy(out=everywhere[:], in_=repeated[:])
 
         w_codes = const.tile([P, HEADS * FEAT], U32, align_bytes=64)
         w_scales = const.tile([P, HEADS * FEAT], U8, align_bytes=64)
@@ -125,39 +124,46 @@ def tile_multiheadattention_pb_kernel(tc, heads, q, proj_w, proj_b, ln_gamma, ln
         residual = {}
         centred = {}
 
-        def prepare(pieces, order, codes, scales):
-            grouped = stage.tile([P, STRIPS * FEAT], BF16, align_bytes=64)
-            places = grouped[:].bitcast(F32).rearrange(order, a=BANK_STRIPS, b=PIECES, u=2)
-            for b in range(PIECES):
+        def prepare(pieces, order, targets):
+            grouped = stage.tile([P, STEP_STRIPS * FEAT], BF16, align_bytes=64)
+            places = grouped[:].bitcast(F32).rearrange(order, a=PIECE_STRIPS, b=STEP_PIECES, u=2)
+            for b in range(STEP_PIECES):
                 words = pieces[b][:].bitcast(F32)
-                bank = banks.tile([P, FEAT], F32, tag="bank")
-                for j in range(BANK_STRIPS * 2):
+                bank = banks.tile([P, FEAT], F32)
+                for j in range(PIECE_STRIPS * 2):
                     nc.tensor.transpose(bank[:, j * P : (j + 1) * P], words[:, j * P : (j + 1) * P], ident[:])
-                nc.scalar.copy(out=places[:, b, :, :, :], in_=bank[:].rearrange("p (a u r) -> p a r u", a=BANK_STRIPS, u=2))
-            for s in range(0, STRIPS, QUANT_STRIPS):
+                nc.scalar.copy(
+                    out=places[:, b, :, :, :], in_=bank[:].rearrange("p (a u r) -> p a r u", a=PIECE_STRIPS, u=2)
+                )
+            width = STEP_STRIPS * FEAT // len(targets)
+            for i, (codes, scales) in enumerate(targets):
                 nc.vector.quantize_mx(
-                    out=codes[:, s * P : (s + QUANT_STRIPS) * P].bitcast(FP8X4),
-                    scales=scales[:, s * P : (s + QUANT_STRIPS) * P],
-                    in_=grouped[:, s * FEAT : (s + QUANT_STRIPS) * FEAT],
+                    out=codes.bitcast(FP8X4), scales=scales, in_=grouped[:, i * width : (i + 1) * width]
                 )
 
-        def prepare_w(c):
-            columns = slice(c * STRIPS * P, (c + 1) * STRIPS * P)
-            prepare(w_raw[c], "p (a b r u) -> p b a r u", w_codes[:, columns], w_scales[:, columns])
+        def prepare_w(pair, step):
+            pieces = [w_raw[(pair, step * STEP_PIECES + b)] for b in range(STEP_PIECES)]
+            targets = []
+            for a in range(PAIR):
+                first = (pair * PAIR + a) * FEAT + step * STEP_PIECES * P
+                columns = slice(first, first + STEP_PIECES * P)
+                targets.append((w_codes[:, columns], w_scales[:, columns]))
+            prepare(pieces, "p (a b r u) -> p b a r u", targets)
 
-        def prepare_x(g, c):
-            x_codes = operands.tile([P, STRIPS * P], U32, align_bytes=64)
-            x_scales = operands.tile([P, STRIPS * P], U8, align_bytes=64)
-            prepare(x_raw[(g, c)], "p (b a r u) -> p b a r u", x_codes[:], x_scales[:])
-            x_operands[(g, c)] = (x_codes, x_scales)
+        def prepare_x(g, pair):
+            pieces = [x_raw[(g, pair, b)] for b in range(PAIR)]
+            x_codes = operands.tile([P, STEP_STRIPS * P], U32, align_bytes=64)
+            x_scales = operands.tile([P, STEP_STRIPS * P], U8, align_bytes=64)
+            prepare(pieces, "p (b a r u) -> p b a r u", [(x_codes[:], x_scales[:])])
+            x_operands[(g, pair)] = (x_codes, x_scales)
 
         def multiply(g, end):
             for t in range(TILES):
                 if heads_done[g] == 0:
                     acc[(g, t)] = sums.tile([P, FEAT], F32, name="acc", tag="acc")
                 for head in range(heads_done[g], end):
-                    x_codes, x_scales = x_operands[(g, head // X_HEADS)]
-                    strip = (head % X_HEADS) * TILES + t
+                    x_codes, x_scales = x_operands[(g, head // PAIR)]
+                    strip = (head % PAIR) * TILES + t
                     nc.tensor.matmul_mx(
                         out=acc[(g, t)][:],
                         lhsT=x_codes[:, strip * P : (strip + 1) * P].bitcast(FP8X4),
@@ -218,26 +224,34 @@ def tile_multiheadattention_pb_kernel(tc, heads, q, proj_w, proj_b, ln_gamma, ln
                 )
                 nc.sync.dma_start(out=group_rows[:, t, :], in_=scaled[:])
 
-        prepare_w(0)
+        for step in range(W_STEPS):
+            prepare_w(0, step)
         prepare_x(0, 0)
-        prepare_w(1)
-        multiply(0, W_HEADS)
-        prepare_w(2)
-        multiply(0, 2 * W_HEADS)
         prepare_x(0, 1)
-        spread_vectors()
-        prepare_w(3)
-        multiply(0, 3 * W_HEADS)
+        for pair in (1, 2):
+            for step in range(W_STEPS):
+                prepare_w(pair, step)
+                multiply(0, heads_done[0] + 1)
+        prepare_x(0, 2)
+        spread_vector(0, bias_all)
+        prepare_x(0, 3)
+        spread_vector(1, gamma_all)
+        for step in range(W_STEPS):
+            prepare_w(3, step)
+            multiply(0, heads_done[0] + 1)
+        spread_vector(2, beta_all)
         add_bias_to_residual(0)
         for g in range(1, GROUPS):
             add_bias_to_residual(g)
             prepare_x(g, 0)
+            prepare_x(g, 1)
             multiply(g - 1, HEADS)
             take_sums(g - 1)
-            prepare_x(g, 1)
+            prepare_x(g, 2)
+            prepare_x(g, 3)
             scale_by_gamma(g - 1)
             normalise_and_store(g - 1)
-            multiply(g, X_HEADS)
+            multiply(g, HEADS // 2)
         multiply(GROUPS - 1, HEADS)
         take_sums(GROUPS - 1)
         scale_by_gamma(GROUPS - 1)

@@ -21,15 +21,14 @@ ROWS = 1024
 FEAT = 512
 LN_EPS = 1e-5
 
-PIECE_STRIPS = 2
-STEP_PIECES = 2
-STEP_STRIPS = STEP_PIECES * PIECE_STRIPS
+STRIPS = 8
+BANK_STRIPS = 2
+PIECES = STRIPS // BANK_STRIPS
+QUANT_STRIPS = 4
 TILES = 2
 GROUPS = ROWS // (TILES * P)
-PAIR = 2
-PAIRS = HEADS // PAIR
-W_BLOCKS = FEAT // P
-W_STEPS = W_BLOCKS // STEP_PIECES
+X_HEADS = STRIPS // TILES
+W_HEADS = STRIPS * P // FEAT
 
 
 def tile_multiheadattention_pb_kernel(tc, heads, q, proj_w, proj_b, ln_gamma, ln_beta, out):
@@ -38,16 +37,14 @@ def tile_multiheadattention_pb_kernel(tc, heads, q, proj_w, proj_b, ln_gamma, ln
     out_rows = out.flatten_outer_dims()
 
     with ExitStack() as ctx:
-        ctx.enter_context(tc.manual_schedule())
         const = ctx.enter_context(tc.tile_pool(name="const", bufs=1))
         raw = ctx.enter_context(tc.tile_pool(name="raw", bufs=1))
-        stage = ctx.enter_context(tc.tile_pool(name="stage", bufs=6))
-        operands = ctx.enter_context(tc.tile_pool(name="operands", bufs=6))
+        stage = ctx.enter_context(tc.tile_pool(name="stage", bufs=3))
+        operands = ctx.enter_context(tc.tile_pool(name="operands", bufs=3))
         rows_pool = ctx.enter_context(tc.tile_pool(name="rows", bufs=4))
         stats = ctx.enter_context(tc.tile_pool(name="stats", bufs=4))
         banks = ctx.enter_context(tc.psum_pool(name="banks", bufs=4))
-        sums = ctx.enter_context(tc.psum_pool(name="sums", bufs=3))
-        spread_pool = ctx.enter_context(tc.psum_pool(name="spread", bufs=1))
+        sums = ctx.enter_context(tc.psum_pool(name="sums", bufs=4))
 
         ident = const.tile([P, P], F32)
         make_identity(nc, ident[:])
@@ -62,28 +59,32 @@ def tile_multiheadattention_pb_kernel(tc, heads, q, proj_w, proj_b, ln_gamma, ln
         warm = const.tile([P, 1], F32)
         nc.scalar.activation(out=warm[:], in_=eps[:], func=INV_SQRT)
 
-        w_raw = {}
+        w_raw = []
         x_raw = {}
         q_raw = []
 
-        def load_w(pair):
-            for b in range(W_BLOCKS):
-                piece = raw.tile([P, PIECE_STRIPS * FEAT], BF16, name="w_raw%d_%d" % (pair, b))
+        def load_w(c):
+            pieces = []
+            for b in range(PIECES):
+                piece = raw.tile([P, BANK_STRIPS * FEAT], BF16, name="w_raw%d_%d" % (c, b))
                 nc.sync.dma_start(
-                    out=piece[:], in_=proj_w[b * P : (b + 1) * P, pair * PAIR * FEAT : (pair + 1) * PAIR * FEAT]
+                    out=piece[:], in_=proj_w[b * P : (b + 1) * P, c * W_HEADS * FEAT : (c + 1) * W_HEADS * FEAT]
                 )
-                w_raw[(pair, b)] = piece
+                pieces.append(piece)
+            w_raw.append(pieces)
 
-        def load_x(g, pair):
-            for b in range(PAIR):
-                piece = raw.tile([P, PIECE_STRIPS * FEAT], BF16, name="x_raw%d_%d_%d" % (g, pair, b))
+        def load_x(g, c):
+            pieces = []
+            for b in range(PIECES):
+                piece = raw.tile([P, BANK_STRIPS * FEAT], BF16, name="x_raw%d_%d_%d" % (g, c, b))
                 nc.sync.dma_start(
                     out=piece[:],
-                    in_=heads[pair * PAIR + b, g * TILES * P : (g + 1) * TILES * P, :].rearrange(
+                    in_=heads[c * X_HEADS + b, g * TILES * P : (g + 1) * TILES * P, :].rearrange(
                         "(p t) d -> p (t d)", t=TILES
                     ),
                 )
-                x_raw[(g, pair, b)] = piece
+                pieces.append(piece)
+            x_raw[(g, c)] = pieces
 
         def load_q(g):
             q_group = raw.tile([P, TILES * FEAT], BF16, name="q_raw%d" % g)
@@ -95,26 +96,25 @@ def tile_multiheadattention_pb_kernel(tc, heads, q, proj_w, proj_b, ln_gamma, ln
 
         load_w(0)
         load_x(0, 0)
-        load_x(0, 1)
         load_w(1)
         load_w(2)
-        load_x(0, 2)
-        load_x(0, 3)
+        load_x(0, 1)
         load_w(3)
         load_q(0)
         for g in range(1, GROUPS):
             load_q(g)
-            for pair in range(PAIRS):
-                load_x(g, pair)
+            load_x(g, 0)
+            load_x(g, 1)
 
         bias_all = const.tile([P, FEAT], F32)
         gamma_all = const.tile([P, FEAT], F32)
         beta_all = const.tile([P, FEAT], F32)
 
-        def spread_vector(j, everywhere):
-            repeated = spread_pool.tile([P, FEAT], F32)
-            nc.tensor.matmul(out=repeated[:], lhsT=ones[:], rhs=vector_rows[:, j, :], start=True, stop=True)
-            nc.vector.tensor_copy(out=everywhere[:], in_=repeated[:])
+        def spread_vectors():
+            for j, spread in enumerate((bias_all, gamma_all, beta_all)):
+                bank = banks.tile([P, FEAT], F32, tag="bank")
+                nc.tensor.matmul(out=bank[:], lhsT=ones[:], rhs=vector_rows[:, j, :], start=True, stop=True)
+                nc.vector.tensor_copy(out=spread[:], in_=bank[:])
 
         w_codes = const.tile([P, HEADS * FEAT], U32, align_bytes=64)
         w_scales = const.tile([P, HEADS * FEAT], U8, align_bytes=64)
@@ -124,46 +124,39 @@ def tile_multiheadattention_pb_kernel(tc, heads, q, proj_w, proj_b, ln_gamma, ln
         residual = {}
         centred = {}
 
-        def prepare(pieces, order, targets):
-            grouped = stage.tile([P, STEP_STRIPS * FEAT], BF16, align_bytes=64)
-            places = grouped[:].bitcast(F32).rearrange(order, a=PIECE_STRIPS, b=STEP_PIECES, u=2)
-            for b in range(STEP_PIECES):
+        def prepare(pieces, order, codes, scales):
+            grouped = stage.tile([P, STRIPS * FEAT], BF16, align_bytes=64)
+            places = grouped[:].bitcast(F32).rearrange(order, a=BANK_STRIPS, b=PIECES, u=2)
+            for b in range(PIECES):
                 words = pieces[b][:].bitcast(F32)
-                bank = banks.tile([P, FEAT], F32)
-                for j in range(PIECE_STRIPS * 2):
+                bank = banks.tile([P, FEAT], F32, tag="bank")
+                for j in range(BANK_STRIPS * 2):
                     nc.tensor.transpose(bank[:, j * P : (j + 1) * P], words[:, j * P : (j + 1) * P], ident[:])
-                nc.scalar.copy(
-                    out=places[:, b, :, :, :], in_=bank[:].rearrange("p (a u r) -> p a r u", a=PIECE_STRIPS, u=2)
-                )
-            width = STEP_STRIPS * FEAT // len(targets)
-            for i, (codes, scales) in enumerate(targets):
+                nc.scalar.copy(out=places[:, b, :, :, :], in_=bank[:].rearrange("p (a u r) -> p a r u", a=BANK_STRIPS, u=2))
+            for s in range(0, STRIPS, QUANT_STRIPS):
                 nc.vector.quantize_mx(
-                    out=codes.bitcast(FP8X4), scales=scales, in_=grouped[:, i * width : (i + 1) * width]
+                    out=codes[:, s * P : (s + QUANT_STRIPS) * P].bitcast(FP8X4),
+                    scales=scales[:, s * P : (s + QUANT_STRIPS) * P],
+                    in_=grouped[:, s * FEAT : (s + QUANT_STRIPS) * FEAT],
                 )
 
-        def prepare_w(pair, step):
-            pieces = [w_raw[(pair, step * STEP_PIECES + b)] for b in range(STEP_PIECES)]
-            targets = []
-            for a in range(PAIR):
-                first = (pair * PAIR + a) * FEAT + step * STEP_PIECES * P
-                columns = slice(first, first + STEP_PIECES * P)
-                targets.append((w_codes[:, columns], w_scales[:, columns]))
-            prepare(pieces, "p (a b r u) -> p b a r u", targets)
+        def prepare_w(c):
+            columns = slice(c * STRIPS * P, (c + 1) * STRIPS * P)
+            prepare(w_raw[c], "p (a b r u) -> p b a r u", w_codes[:, columns], w_scales[:, columns])
 
-        def prepare_x(g, pair):
-            pieces = [x_raw[(g, pair, b)] for b in range(PAIR)]
-            x_codes = operands.tile([P, STEP_STRIPS * P], U32, align_bytes=64)
-            x_scales = operands.tile([P, STEP_STRIPS * P], U8, align_bytes=64)
-            prepare(pieces, "p (b a r u) -> p b a r u", [(x_codes[:], x_scales[:])])
-            x_operands[(g, pair)] = (x_codes, x_scales)
+        def prepare_x(g, c):
+            x_codes = operands.tile([P, STRIPS * P], U32, align_bytes=64)
+            x_scales = operands.tile([P, STRIPS * P], U8, align_bytes=64)
+            prepare(x_raw[(g, c)], "p (b a r u) -> p b a r u", x_codes[:], x_scales[:])
+            x_operands[(g, c)] = (x_codes, x_scales)
 
         def multiply(g, end):
             for t in range(TILES):
                 if heads_done[g] == 0:
                     acc[(g, t)] = sums.tile([P, FEAT], F32, name="acc", tag="acc")
                 for head in range(heads_done[g], end):
-                    x_codes, x_scales = x_operands[(g, head // PAIR)]
-                    strip = (head % PAIR) * TILES + t
+                    x_codes, x_scales = x_operands[(g, head // X_HEADS)]
+                    strip = (head % X_HEADS) * TILES + t
                     nc.tensor.matmul_mx(
                         out=acc[(g, t)][:],
                         lhsT=x_codes[:, strip * P : (strip + 1) * P].bitcast(FP8X4),
@@ -224,34 +217,26 @@ def tile_multiheadattention_pb_kernel(tc, heads, q, proj_w, proj_b, ln_gamma, ln
                 )
                 nc.sync.dma_start(out=group_rows[:, t, :], in_=scaled[:])
 
-        for step in range(W_STEPS):
-            prepare_w(0, step)
+        prepare_w(0)
         prepare_x(0, 0)
+        prepare_w(1)
+        multiply(0, W_HEADS)
+        prepare_w(2)
+        multiply(0, 2 * W_HEADS)
         prepare_x(0, 1)
-        for pair in (1, 2):
-            for step in range(W_STEPS):
-                prepare_w(pair, step)
-                multiply(0, heads_done[0] + 1)
-        prepare_x(0, 2)
-        spread_vector(0, bias_all)
-        prepare_x(0, 3)
-        spread_vector(1, gamma_all)
-        for step in range(W_STEPS):
-            prepare_w(3, step)
-            multiply(0, heads_done[0] + 1)
-        spread_vector(2, beta_all)
+        spread_vectors()
+        prepare_w(3)
+        multiply(0, 3 * W_HEADS)
         add_bias_to_residual(0)
         for g in range(1, GROUPS):
             add_bias_to_residual(g)
             prepare_x(g, 0)
-            prepare_x(g, 1)
             multiply(g - 1, HEADS)
             take_sums(g - 1)
-            prepare_x(g, 2)
-            prepare_x(g, 3)
+            prepare_x(g, 1)
             scale_by_gamma(g - 1)
             normalise_and_store(g - 1)
-            multiply(g, HEADS // 2)
+            multiply(g, X_HEADS)
         multiply(GROUPS - 1, HEADS)
         take_sums(GROUPS - 1)
         scale_by_gamma(GROUPS - 1)

from contextlib import ExitStack

import concourse.mybir as mybir
from concourse.masks import make_identity

FLOPS = 2 * 1024 * 4096 * 512

F32 = mybir.dt.float32
BF16 = mybir.dt.bfloat16
U32 = mybir.dt.uint32
U8 = mybir.dt.uint8
FP8X4 = mybir.dt.float8_e4m3fn_x4
ADD = mybir.AluOpType.add
MULT = mybir.AluOpType.mult
SQUARE = mybir.ActivationFunctionType.Square
INV_SQRT = mybir.ActivationFunctionType.Abs_reciprocal_sqrt

P = 128
HEADS = 8
ROWS = 1024
FEAT = 512
LN_EPS = 1e-5

STRIPS = 8
BANK_STRIPS = 2
PIECES = STRIPS // BANK_STRIPS
QUANT_STRIPS = 4
TILES = 2
GROUPS = ROWS // (TILES * P)
X_HEADS = STRIPS // TILES
W_HEADS = STRIPS * P // FEAT


def tile_multiheadattention_pb_kernel(tc, heads, q, proj_w, proj_b, ln_gamma, ln_beta, out):
    nc = tc.nc
    q_rows = q.flatten_outer_dims()
    out_rows = out.flatten_outer_dims()

    with ExitStack() as ctx:
        const = ctx.enter_context(tc.tile_pool(name="const", bufs=1))
        raw = ctx.enter_context(tc.tile_pool(name="raw", bufs=1))
        stage = ctx.enter_context(tc.tile_pool(name="stage", bufs=3))
        operands = ctx.enter_context(tc.tile_pool(name="operands", bufs=3))
        rows_pool = ctx.enter_context(tc.tile_pool(name="rows", bufs=4))
        stats = ctx.enter_context(tc.tile_pool(name="stats", bufs=4))
        banks = ctx.enter_context(tc.psum_pool(name="banks", bufs=4))
        sums = ctx.enter_context(tc.psum_pool(name="sums", bufs=4))

        ident = const.tile([P, P], F32)
        make_identity(nc, ident[:])
        ones = const.tile([P, P], BF16)
        nc.vector.memset(ones[:], 1.0)
        eps = const.tile([P, 1], F32)
        nc.vector.memset(eps[:], LN_EPS)
        vector_rows = const.tile([P, 3, FEAT], BF16)
        nc.vector.memset(vector_rows[:], 0.0)
        for j, vector in enumerate((proj_b, ln_gamma, ln_beta)):
            nc.scalar.dma_start(out=vector_rows[0:1, j, :], in_=vector.rearrange("(o n) -> o n", o=1))
        warm = const.tile([P, 1], F32)
        nc.scalar.activation(out=warm[:], in_=eps[:], func=INV_SQRT)

        w_raw = []
        x_raw = {}
        q_raw = []

        def load_w(c):
            pieces = []
            for b in range(PIECES):
                piece = raw.tile([P, BANK_STRIPS * FEAT], BF16, name="w_raw%d_%d" % (c, b))
                nc.sync.dma_start(
                    out=piece[:], in_=proj_w[b * P : (b + 1) * P, c * W_HEADS * FEAT : (c + 1) * W_HEADS * FEAT]
                )
                pieces.append(piece)
            w_raw.append(pieces)

        def load_x(g, c):
            pieces = []
            for b in range(PIECES):
                piece = raw.tile([P, BANK_STRIPS * FEAT], BF16, name="x_raw%d_%d_%d" % (g, c, b))
                nc.sync.dma_start(
                    out=piece[:],
                    in_=heads[c * X_HEADS + b, g * TILES * P : (g + 1) * TILES * P, :].rearrange(
                        "(p t) d -> p (t d)", t=TILES
                    ),
                )
                pieces.append(piece)
            x_raw[(g, c)] = pieces

        def load_q(g):
            q_group = raw.tile([P, TILES * FEAT], BF16, name="q_raw%d" % g)
            nc.sync.dma_start(
                out=q_group[:],
                in_=q_rows[g * TILES * P : (g + 1) * TILES * P, :].rearrange("(p t) n -> p (t n)", t=TILES),
            )
            q_raw.append(q_group)

        load_w(0)
        load_x(0, 0)
        load_w(1)
        load_w(2)
        load_x(0, 1)
        load_w(3)
        load_q(0)
        for g in range(1, GROUPS):
            load_q(g)
            load_x(g, 0)
            load_x(g, 1)

        bias_all = const.tile([P, FEAT], F32)
        gamma_all = const.tile([P, FEAT], F32)
        beta_all = const.tile([P, FEAT], F32)

        def spread_vectors():
            for j, spread in enumerate((bias_all, gamma_all, beta_all)):
                bank = banks.tile([P, FEAT], F32, tag="bank")
                nc.tensor.matmul(out=bank[:], lhsT=ones[:], rhs=vector_rows[:, j, :], start=True, stop=True)
                nc.vector.tensor_copy(out=spread[:], in_=bank[:])

        w_codes = const.tile([P, HEADS * FEAT], U32, align_bytes=64)
        w_scales = const.tile([P, HEADS * FEAT], U8, align_bytes=64)
        x_operands = {}
        heads_done = [0] * GROUPS
        acc = {}
        residual = {}
        centred = {}

        def prepare(pieces, order, codes, scales):
            grouped = stage.tile([P, STRIPS * FEAT], BF16, align_bytes=64)
            places = grouped[:].bitcast(F32).rearrange(order, a=BANK_STRIPS, b=PIECES, u=2)
            for b in range(PIECES):
                words = pieces[b][:].bitcast(F32)
                bank = banks.tile([P, FEAT], F32, tag="bank")
                for j in range(BANK_STRIPS * 2):
                    nc.tensor.transpose(bank[:, j * P : (j + 1) * P], words[:, j * P : (j + 1) * P], ident[:])
                nc.scalar.copy(out=places[:, b, :, :, :], in_=bank[:].rearrange("p (a u r) -> p a r u", a=BANK_STRIPS, u=2))
            for s in range(0, STRIPS, QUANT_STRIPS):
                nc.vector.quantize_mx(
                    out=codes[:, s * P : (s + QUANT_STRIPS) * P].bitcast(FP8X4),
                    scales=scales[:, s * P : (s + QUANT_STRIPS) * P],
                    in_=grouped[:, s * FEAT : (s + QUANT_STRIPS) * FEAT],
                )

        def prepare_w(c):
            columns = slice(c * STRIPS * P, (c + 1) * STRIPS * P)
            prepare(w_raw[c], "p (a b r u) -> p b a r u", w_codes[:, columns], w_scales[:, columns])

        def prepare_x(g, c):
            x_codes = operands.tile([P, STRIPS * P], U32, align_bytes=64)
            x_scales = operands.tile([P, STRIPS * P], U8, align_bytes=64)
            prepare(x_raw[(g, c)], "p (b a r u) -> p b a r u", x_codes[:], x_scales[:])
            x_operands[(g, c)] = (x_codes, x_scales)

        def multiply(g, end):
            for t in range(TILES):
                if heads_done[g] == 0:
                    acc[(g, t)] = sums.tile([P, FEAT], F32, name="acc", tag="acc")
                for head in range(heads_done[g], end):
                    x_codes, x_scales = x_operands[(g, head // X_HEADS)]
                    strip = (head % X_HEADS) * TILES + t
                    nc.tensor.matmul_mx(
                        out=acc[(g, t)][:],
                        lhsT=x_codes[:, strip * P : (strip + 1) * P].bitcast(FP8X4),
                        lhsT_scale=x_scales[:, strip * P : (strip + 1) * P],
                        rhs=w_codes[:, head * FEAT : (head + 1) * FEAT].bitcast(FP8X4),
                        rhs_scale=w_scales[:, head * FEAT : (head + 1) * FEAT],
                        start=(head == 0),
                        stop=(head == HEADS - 1),
                    )
            heads_done[g] = end

        def add_bias_to_residual(g):
            q_plus_b = rows_pool.tile([P, TILES, FEAT], F32, bufs=2)
            nc.vector.tensor_tensor(
                out=q_plus_b[:],
                in0=q_raw[g][:].rearrange("p (t n) -> p t n", t=TILES),
                in1=bias_all[:].unsqueeze(1).to_broadcast([P, TILES, FEAT]),
                op=ADD,
            )
            residual[g] = q_plus_b

        def take_sums(g):
            for t in range(TILES):
                x = rows_pool.tile([P, FEAT], F32)
                row_sum = stats.tile([P, 1], F32)
                nc.vector.scalar_tensor_tensor(
                    out=x[:], in0=acc[(g, t)][:], scalar=0.0, in1=residual[g][:, t, :], op0=ADD, op1=ADD,
                    accum_out=row_sum[:],
                )
                minus_mean = stats.tile([P, 1], F32)
                nc.gpsimd.tensor_scalar(
                    out=minus_mean[:], in0=row_sum[:], scalar1=-1.0 / FEAT, scalar2=0.0, op0=MULT, op1=ADD
                )
                centred[(g, t)] = (x, minus_mean)

        def scale_by_gamma(g):
            for t in range(TILES):
                x, minus_mean = centred[(g, t)]
                scaled = rows_pool.tile([P, FEAT], F32)
                nc.vector.scalar_tensor_tensor(
                    out=scaled[:], in0=x[:], scalar=minus_mean[:], in1=gamma_all[:], op0=ADD, op1=MULT
                )
                centred[(g, t)] = (x, minus_mean, scaled)

        def normalise_and_store(g):
            group_rows = out_rows[g * TILES * P : (g + 1) * TILES * P, :].rearrange("(p t) n -> p t n", t=TILES)
            for t in range(TILES):
                x, minus_mean, scaled = centred[(g, t)]
                squares = rows_pool.tile([P, FEAT], F32, bufs=2)
                square_sum = stats.tile([P, 1], F32)
                nc.scalar.activation(
                    out=squares[:], in_=x[:], func=SQUARE, bias=minus_mean[:], scale=1.0, accum_out=square_sum[:]
                )
                inverse = stats.tile([P, 1], F32)
                nc.scalar.activation(out=inverse[:], in_=square_sum[:], func=INV_SQRT, bias=eps[:], scale=1.0 / FEAT)
                nc.vector.scalar_tensor_tensor(
                    out=scaled[:], in0=scaled[:], scalar=inverse[:], in1=beta_all[:], op0=MULT, op1=ADD
                )
                nc.sync.dma_start(out=group_rows[:, t, :], in_=scaled[:])

        prepare_w(0)
        prepare_x(0, 0)
        prepare_w(1)
        multiply(0, W_HEADS)
        prepare_w(2)
        multiply(0, 2 * W_HEADS)
        prepare_x(0, 1)
        spread_vectors()
        prepare_w(3)
        multiply(0, 3 * W_HEADS)
        add_bias_to_residual(0)
        for g in range(1, GROUPS):
            add_bias_to_residual(g)
            prepare_x(g, 0)
            multiply(g - 1, HEADS)
            take_sums(g - 1)
            prepare_x(g, 1)
            scale_by_gamma(g - 1)
            normalise_and_store(g - 1)
            multiply(g, X_HEADS)
        multiply(GROUPS - 1, HEADS)
        take_sums(GROUPS - 1)
        scale_by_gamma(GROUPS - 1)
        normalise_and_store(GROUPS - 1)
